import numpy as np
import ml_dtypes


def mxq(x, axis, fmt="e4m3"):
    dtype, down = {"e4m3": (ml_dtypes.float8_e4m3fn, 7), "e5m2": (ml_dtypes.float8_e5m2, 14)}[fmt]
    v = np.moveaxis(np.asarray(x, np.float32).astype(ml_dtypes.bfloat16).astype(np.float64), axis, -1)
    blocks = v.reshape(v.shape[:-1] + (-1, 32))
    amax = np.abs(blocks).max(-1, keepdims=True)
    byte = np.maximum(np.where(amax > 0, np.frexp(amax)[1] - 1 + 127, 0) - down, 1)
    scale = np.exp2(byte - 127.0)
    codes = (blocks / scale).astype(np.float32).astype(dtype).astype(np.float64)
    return np.moveaxis((codes * scale).reshape(v.shape), -1, axis)


WIDE = False


def mx_kscale(k):
    if not WIDE:
        return np.ones(k)
    levels = np.array([10, -10, 5, -5, 0])
    a = np.random.permutation(np.resize(levels, k // 512 * 4)).reshape(k // 512, 4)
    idx = np.arange(k)
    return np.exp2(a[idx // 512, idx % 128 // 32])


BF16 = ml_dtypes.bfloat16


def bf(x):
    return np.asarray(x, np.float32).astype(BF16)


def f64(x):
    return np.asarray(x).astype(np.float64)


E2M1 = np.array([0.0, 0.5, 1.0, 1.5, 2.0, 3.0, 4.0, 6.0, -0.0, -0.5, -1.0, -1.5, -2.0, -3.0, -4.0, -6.0])


def pack_weight(w, fmt):
    k, n = w.shape
    w = f64(bf(w)).reshape(k // 32, 32, n)
    amax = np.abs(w).max(1)
    if fmt == "e4m3":
        byte = np.frexp(amax)[1] - 1 + 127 - 7
    else:
        mant, ex = np.frexp(amax / 6.0)
        byte = np.where(mant > 0.5, ex, ex - 1) + 127
    byte = np.clip(np.where(amax > 0, byte, 1), 1, 254)
    scaled = (w * np.exp2(127.0 - byte)[:, None, :]).reshape(k, n).astype(np.float32)
    by_word = np.ascontiguousarray(scaled.reshape(k // 512, 128, 4, n).transpose(0, 1, 3, 2))
    if fmt == "e4m3":
        words = by_word.astype(ml_dtypes.float8_e4m3fn).view(np.uint8)
    else:
        c = by_word.astype(ml_dtypes.float4_e2m1fn).view(np.uint8) & 0xF
        words = c[..., 0::2] | (c[..., 1::2] << 4)
    return np.ascontiguousarray(words), np.ascontiguousarray(byte.astype(np.uint8).reshape(k // 512, 16, n))


def unpack_weight(words, scales, fmt):
    g, p, n, _ = words.shape
    if fmt == "e4m3":
        vals = np.ascontiguousarray(words).view(ml_dtypes.float8_e4m3fn).astype(np.float64)
    else:
        nib = np.empty((g, p, n, 4), np.uint8)
        nib[..., 0::2] = words & 0xF
        nib[..., 1::2] = words >> 4
        vals = E2M1[nib]
    vals = vals * np.repeat(np.exp2(scales.astype(np.float64) - 127.0), 8, axis=1)[..., None]
    return vals.transpose(0, 1, 3, 2).reshape(g * 512, n)

def pack4(w):
    words, scales = pack_weight(w, "e2m1")
    return words.reshape(words.shape[0], 128, -1), scales


def unpack4(words, scales):
    return unpack_weight(words.reshape(words.shape[0], 128, -1, 2), scales, "e2m1")


B, S, HID, H, HK, D = 4, 2048, 512, 2, 2, 64
EPS = 1e-6
PRE = 0.004


def rmsnorm(v, w):
    var = np.mean(v * v, axis=-1, keepdims=True)
    return w * (v * (1.0 / np.sqrt(var + EPS)))


def rope(v, cos, sin):
    c = cos[:, :, None, :]
    sn = sin[:, :, None, :]
    v1, v2 = np.split(v, 2, axis=-1)
    rot = np.concatenate([-v2, v1], axis=-1)
    return v * c + rot * sn


def setup_inputs():
    s = mx_kscale(HID)
    hidden_states = bf(np.random.standard_normal((B, S, HID)) * s)
    cos = bf(np.cos(np.random.standard_normal((B, S, D))))
    sin = bf(np.sin(np.random.standard_normal((B, S, D))))
    wq = np.random.standard_normal((H * D, HID)) * PRE / np.sqrt(HID) / s
    wk = np.random.standard_normal((HK * D, HID)) * PRE / np.sqrt(HID) / s
    q_norm_w = bf(1.0 + 0.1 * np.random.standard_normal(D))
    k_norm_w = bf(1.0 + 0.1 * np.random.standard_normal(D))
    wq_words, wq_scales = pack4(np.ascontiguousarray(wq.T))
    wk_words, wk_scales = pack4(np.ascontiguousarray(wk.T))
    return {
        "hidden_states": hidden_states,
        "cos": cos,
        "sin": sin,
        "Wq_query_words": wq_words,
        "Wq_query_scales": wq_scales,
        "Wk_words": wk_words,
        "Wk_scales": wk_scales,
        "q_norm_w": q_norm_w,
        "k_norm_w": k_norm_w,
    }


def reference(hidden_states, cos, sin, Wq_query_words, Wq_query_scales, Wk_words, Wk_scales, q_norm_w, k_norm_w):
    xq = mxq(f64(hidden_states), 2, "e4m3")
    q = (xq @ unpack4(Wq_query_words, Wq_query_scales)).reshape(B, S, H, D)
    k = (xq @ unpack4(Wk_words, Wk_scales)).reshape(B, S, HK, D)
    q = rmsnorm(q, f64(q_norm_w))
    k = rmsnorm(k, f64(k_norm_w))
    q = rope(q, f64(cos), f64(sin))
    k = rope(k, f64(cos), f64(sin))
    return q, k

@@ -1,0 +1,253 @@
+from contextlib import ExitStack
+
+import concourse.mybir as mybir
+from concourse.masks import make_identity
+
+F32 = mybir.dt.float32
+BF16 = mybir.dt.bfloat16
+U8 = mybir.dt.uint8
+U32 = mybir.dt.uint32
+I32 = mybir.dt.int32
+FP8X4 = mybir.dt.float8_e4m3fn_x4
+FP4X4 = mybir.dt.float4_e2m1fn_x4
+ALU = mybir.AluOpType
+ACT = mybir.ActivationFunctionType
+
+P = 128
+PACK = 4
+K = P * PACK
+TOKENS = 4 * 2048
+TILES = TOKENS // P
+HEADS = 2
+D = 64
+HALF = D // 2
+SIDES = 2
+N_SIDE = HEADS * D
+N_OUT = SIDES * N_SIDE
+EPS = 1e-6
+
+PAIR = 2
+CHUNK = 8
+PAIRS = TILES // PAIR
+PAIRS_IN_CHUNK = CHUNK // PAIR
+CHUNKS = TILES // CHUNK
+GROUPS = PAIR * SIDES * HEADS
+
+FLOPS = 2 * TOKENS * K * N_OUT
+
+
+def tile_qwen3nextattentionforengine_pa_t_kernel(
+    tc,
+    hidden_states,
+    cos,
+    sin,
+    Wq_query_words,
+    Wq_query_scales,
+    Wk_words,
+    Wk_scales,
+    q_norm_w,
+    k_norm_w,
+    out_0,
+    out_1,
+):
+    nc = tc.nc
+    x_view = hidden_states.rearrange("b (q i) k -> (b q) i k", i=TILES)
+    cos_view = cos.rearrange("b (q i) d -> (b q) i d", i=TILES)
+    sin_view = sin.rearrange("b (q i) d -> (b q) i d", i=TILES)
+    out_views = (
+        out_0.rearrange("b (q i) h d -> (b q) i (h d)", i=TILES),
+        out_1.rearrange("b (q i) h d -> (b q) i (h d)", i=TILES),
+    )
+
+    with ExitStack() as pools:
+        const = pools.enter_context(tc.tile_pool(name="const", bufs=1))
+        x_pool = pools.enter_context(tc.tile_pool(name="x_pool", bufs=3))
+        table_pool = pools.enter_context(tc.tile_pool(name="table_pool", bufs=3))
+        quant_pool = pools.enter_context(tc.tile_pool(name="quant_pool", bufs=3))
+        stat_pool = pools.enter_context(tc.tile_pool(name="stat_pool", bufs=4))
+        prod_pool = pools.enter_context(tc.tile_pool(name="prod_pool", bufs=3))
+        res_pool = pools.enter_context(tc.tile_pool(name="res_pool", bufs=3))
+        xt_psum = pools.enter_context(tc.psum_pool(name="xt_psum", bufs=3))
+        v_psum = pools.enter_context(tc.psum_pool(name="v_psum", bufs=5))
+        pools.enter_context(tc.manual_schedule())
+
+        x_chunks = {}
+
+        def load_x(c, pieces):
+            x_sb = x_pool.tile([P, CHUNK, K], BF16, name="x_sb")
+            step = CHUNK // pieces
+            for first in range(0, CHUNK, step):
+                nc.sync.dma_start(
+                    out=x_sb[:, first : first + step, :],
+                    in_=x_view[:, c * CHUNK + first : c * CHUNK + first + step, :],
+                )
+            x_chunks[c] = x_sb
+
+        gains = const.tile([P, SIDES, 2, D], BF16, name="gains")
+        nc.scalar.dma_start(out=gains[:, 0, 0, :], in_=q_norm_w.partition_broadcast(P))
+        nc.scalar.dma_start(out=gains[:, 1, 0, :], in_=k_norm_w.partition_broadcast(P))
+        cos_sb = const.tile([P, TILES, D], BF16, name="cos_sb")
+        sin_sb = const.tile([P, TILES, D], BF16, name="sin_sb")
+        nc.sync.dma_start(out=cos_sb[:, 0:CHUNK, :], in_=cos_view[:, 0:CHUNK, :])
+        nc.sync.dma_start(out=sin_sb[:, 0:CHUNK, :], in_=sin_view[:, 0:CHUNK, :])
+        load_x(0, 2)
+
+        ident = const.tile([P, P], F32, name="ident")
+        make_identity(nc, ident[:])
+        eps = const.tile([P, 1], F32, name="eps")
+        nc.vector.memset(eps[:], EPS)
+
+        w_words = const.tile([P, 2 * N_OUT], U8, name="w_words", align_bytes=64)
+        w_plane = const.tile([P, N_OUT], U8, name="w_plane", align_bytes=64)
+        nc.vector.memset(w_plane[:].bitcast(I32), 0)
+        for s, words in enumerate((Wq_query_words, Wk_words)):
+            nc.sync.dma_start(
+                out=w_words[:, s * 2 * N_SIDE : (s + 1) * 2 * N_SIDE].bitcast(I32),
+                in_=words.rearrange("g p n -> (g p) n").bitcast(I32),
+            )
+        for s, scales in enumerate((Wq_query_scales, Wk_scales)):
+            rows = scales.rearrange("g q n -> (g q) n")
+            for quad in range(4):
+                nc.sync.dma_start(
+                    out=w_plane[32 * quad : 32 * quad + 4, s * N_SIDE : (s + 1) * N_SIDE].bitcast(I32),
+                    in_=rows[4 * quad : 4 * quad + 4, :].bitcast(I32),
+                )
+
+        load_x(1, 1)
+        nc.sync.dma_start(out=cos_sb[:, CHUNK:TILES, :], in_=cos_view[:, CHUNK:TILES, :])
+        nc.sync.dma_start(out=sin_sb[:, CHUNK:TILES, :], in_=sin_view[:, CHUNK:TILES, :])
+
+        nc.vector.tensor_copy(out=gains[:, :, 1, 0:HALF], in_=gains[:, :, 0, 0:HALF])
+        nc.vector.tensor_scalar_mul(out=gains[:, :, 1, HALF:D], in0=gains[:, :, 0, HALF:D], scalar1=-1.0)
+
+        tables = {}
+
+        def build_tables(c):
+            tiles = slice(c * CHUNK, (c + 1) * CHUNK)
+            table = table_pool.tile([P, CHUNK, SIDES, 2, D], F32, name="table")
+            nc.gpsimd.tensor_tensor(
+                out=table[:, :, :, 0, :],
+                in0=cos_sb[:, tiles, :].unsqueeze(2).to_broadcast([P, CHUNK, SIDES, D]),
+                in1=gains[:, :, 0, :].unsqueeze(1).to_broadcast([P, CHUNK, SIDES, D]),
+                op=ALU.mult,
+            )
+            for a in range(2):
+                mine = slice(a * HALF, (a + 1) * HALF)
+                other = slice((1 - a) * HALF, (2 - a) * HALF)
+                nc.gpsimd.tensor_tensor(
+                    out=table[:, :, :, 1, mine],
+                    in0=sin_sb[:, tiles, other].unsqueeze(2).to_broadcast([P, CHUNK, SIDES, HALF]),
+                    in1=gains[:, :, 1, mine].unsqueeze(1).to_broadcast([P, CHUNK, SIDES, HALF]),
+                    op=ALU.mult,
+                )
+            tables[c] = table
+
+        transposed = {}
+
+        def transpose(j):
+            x_sb = x_chunks[j // PAIRS_IN_CHUNK]
+            xt = xt_psum.tile([P, PAIR, 2, P], F32, name="xt")
+            for t in range(PAIR):
+                words = x_sb[:, (j % PAIRS_IN_CHUNK) * PAIR + t, :].bitcast(F32)
+                for u in range(2):
+                    nc.tensor.transpose(xt[:, t, u, :], words[:, u : K // 2 : 2], ident[:])
+            grouped = quant_pool.tile([P, PAIR * P * PACK], BF16, name="grouped", align_bytes=64)
+            nc.scalar.copy(
+                out=grouped[:].bitcast(F32).rearrange("p (t r u) -> p t r u", t=PAIR, u=2),
+                in_=xt[:].rearrange("p t u r -> p t r u"),
+            )
+            transposed[j] = grouped
+
+        quantised = {}
+
+        def quantise(j):
+            grouped = transposed.pop(j)
+            codes = quant_pool.tile([P, PAIR * P], U32, name="codes", align_bytes=64)
+            plane = quant_pool.tile([P, PAIR * P], U8, name="plane", align_bytes=64)
+            nc.vector.quantize_mx(out=codes[:].bitcast(FP8X4), scales=plane[:], in_=grouped[:])
+            quantised[j] = (codes, plane)
+
+        projected = {}
+
+        def project_and_measure(j):
+            codes, plane = quantised.pop(j)
+            v = v_psum.tile([P, PAIR, N_OUT], F32, name="v")
+            for t in range(PAIR):
+                tokens = slice(t * P, (t + 1) * P)
+                nc.tensor.matmul_mx(
+                    out=v[:, t, :],
+                    lhsT=codes[:, tokens].bitcast(FP8X4),
+                    lhsT_scale=plane[:, tokens],
+                    rhs=w_words[:].bitcast(FP4X4),
+                    rhs_scale=w_plane[:],
+                    start=True,
+                    stop=True,
+                )
+            heads = v[:].rearrange("p t (g d) -> p (t g) d", d=D)
+            sumsq = stat_pool.tile([P, GROUPS], F32, name="sumsq")
+            for g in range(GROUPS):
+                squares = stat_pool.tile([P, D], F32, name="squares")
+                nc.scalar.activation(
+                    out=squares[:], in_=heads[:, g, :], func=ACT.Square, accum_out=sumsq[:, g : g + 1]
+                )
+            rstd = stat_pool.tile([P, GROUPS], F32, name="rstd")
+            nc.scalar.activation(
+                out=rstd[:], in_=sumsq[:], func=ACT.Abs_reciprocal_sqrt, bias=eps[:, 0:1], scale=1.0 / D
+            )
+            projected[j] = (heads, rstd)
+
+        products = {}
+
+        def multiply(j):
+            heads, rstd = projected.pop(j)
+            first = (j % PAIRS_IN_CHUNK) * PAIR
+            table = tables[j // PAIRS_IN_CHUNK]
+            prod = prod_pool.tile([P, SIDES, PAIR, HEADS, 2, D], F32, name="prod")
+            for t in range(PAIR):
+                for s in range(SIDES):
+                    for h in range(HEADS):
+                        g = (t * SIDES + s) * HEADS + h
+                        nc.vector.scalar_tensor_tensor(
+                            out=prod[:, s, t, h, :, :],
+                            in0=heads[:, g, :].unsqueeze(1).to_broadcast([P, 2, D]),
+                            scalar=rstd[:, g : g + 1],
+                            in1=table[:, first + t, s, :, :],
+                            op0=ALU.mult,
+                            op1=ALU.mult,
+                        )
+            products[j] = prod
+
+        def add_and_store(j):
+            prod = products.pop(j)
+            res = res_pool.tile([P, SIDES, PAIR, HEADS, 2, HALF], F32, name="res")
+            for a in range(2):
+                nc.vector.tensor_tensor(
+                    out=res[:, :, :, :, a, :],
+                    in0=prod[:, :, :, :, 0, a * HALF : (a + 1) * HALF],
+                    in1=prod[:, :, :, :, 1, (1 - a) * HALF : (2 - a) * HALF],
+                    op=ALU.add,
+                )
+            for s in range(SIDES):
+                nc.sync.dma_start(
+                    out=out_views[s][:, j * PAIR : (j + 1) * PAIR, :],
+                    in_=res[:, s].rearrange("p i h a d -> p i (h a d)"),
+                )
+
+        build_tables(0)
+        for i in range(-4, PAIRS):
+            if i + 4 < PAIRS:
+                if (i + 4) % PAIRS_IN_CHUNK == 0:
+                    c = (i + 4) // PAIRS_IN_CHUNK
+                    if c + 2 < CHUNKS:
+                        load_x(c + 2, 1)
+                    if c + 1 < CHUNKS:
+                        build_tables(c + 1)
+                transpose(i + 4)
+            if 0 <= i + 2 < PAIRS:
+                project_and_measure(i + 2)
+            if i >= 0:
+                multiply(i)
+            if 0 <= i + 3 < PAIRS:
+                quantise(i + 3)
+            if i >= 0:
+                add_and_store(i)

@@ -62,7 +62,7 @@ def tile_qwen3nextattentionforengine_pa_t_kernel(
     with ExitStack() as pools:
         const = pools.enter_context(tc.tile_pool(name="const", bufs=1))
         x_pool = pools.enter_context(tc.tile_pool(name="x_pool", bufs=3))
-        table_pool = pools.enter_context(tc.tile_pool(name="table_pool", bufs=3))
+        table_pool = pools.enter_context(tc.tile_pool(name="table_pool", bufs=4))
         quant_pool = pools.enter_context(tc.tile_pool(name="quant_pool", bufs=3))
         stat_pool = pools.enter_context(tc.tile_pool(name="stat_pool", bufs=4))
         prod_pool = pools.enter_context(tc.tile_pool(name="prod_pool", bufs=3))
@@ -86,10 +86,15 @@ def tile_qwen3nextattentionforengine_pa_t_kernel(
         gains = const.tile([P, SIDES, 2, D], BF16, name="gains")
         nc.scalar.dma_start(out=gains[:, 0, 0, :], in_=q_norm_w.partition_broadcast(P))
         nc.scalar.dma_start(out=gains[:, 1, 0, :], in_=k_norm_w.partition_broadcast(P))
-        cos_sb = const.tile([P, TILES, D], BF16, name="cos_sb")
-        sin_sb = const.tile([P, TILES, D], BF16, name="sin_sb")
-        nc.sync.dma_start(out=cos_sb[:, 0:CHUNK, :], in_=cos_view[:, 0:CHUNK, :])
-        nc.sync.dma_start(out=sin_sb[:, 0:CHUNK, :], in_=sin_view[:, 0:CHUNK, :])
+        angles = const.tile([P, TILES, 2, D], BF16, name="angles")
+
+        def load_angles(c):
+            tiles = slice(c * CHUNK, (c + 1) * CHUNK)
+            nc.sync.dma_start(out=angles[:, tiles, 0, :], in_=cos_view[:, tiles, :])
+            nc.sync.dma_start(out=angles[:, tiles, 1, 0:HALF], in_=sin_view[:, tiles, HALF:D])
+            nc.sync.dma_start(out=angles[:, tiles, 1, HALF:D], in_=sin_view[:, tiles, 0:HALF])
+
+        load_angles(0)
         load_x(0, 2)
 
         ident = const.tile([P, P], F32, name="ident")
@@ -114,33 +119,25 @@ def tile_qwen3nextattentionforengine_pa_t_kernel(
                 )
 
         load_x(1, 1)
-        nc.sync.dma_start(out=cos_sb[:, CHUNK:TILES, :], in_=cos_view[:, CHUNK:TILES, :])
-        nc.sync.dma_start(out=sin_sb[:, CHUNK:TILES, :], in_=sin_view[:, CHUNK:TILES, :])
+        load_angles(1)
 
         nc.vector.tensor_copy(out=gains[:, :, 1, 0:HALF], in_=gains[:, :, 0, 0:HALF])
         nc.vector.tensor_scalar_mul(out=gains[:, :, 1, HALF:D], in0=gains[:, :, 0, HALF:D], scalar1=-1.0)
 
         tables = {}
 
-        def build_tables(c):
-            tiles = slice(c * CHUNK, (c + 1) * CHUNK)
-            table = table_pool.tile([P, CHUNK, SIDES, 2, D], F32, name="table")
+        def build_table(j):
+            table = table_pool.tile([P, PAIR, SIDES, 2 * D], F32, name="table")
             nc.gpsimd.tensor_tensor(
-                out=table[:, :, :, 0, :],
-                in0=cos_sb[:, tiles, :].unsqueeze(2).to_broadcast([P, CHUNK, SIDES, D]),
-                in1=gains[:, :, 0, :].unsqueeze(1).to_broadcast([P, CHUNK, SIDES, D]),
+                out=table[:],
+                in0=angles[:, j * PAIR : (j + 1) * PAIR, :, :]
+                .rearrange("p t c d -> p t (c d)")
+                .unsqueeze(2)
+                .to_broadcast([P, PAIR, SIDES, 2 * D]),
+                in1=gains[:].rearrange("p s c d -> p s (c d)").unsqueeze(1).to_broadcast([P, PAIR, SIDES, 2 * D]),
                 op=ALU.mult,
             )
-            for a in range(2):
-                mine = slice(a * HALF, (a + 1) * HALF)
-                other = slice((1 - a) * HALF, (2 - a) * HALF)
-                nc.gpsimd.tensor_tensor(
-                    out=table[:, :, :, 1, mine],
-                    in0=sin_sb[:, tiles, other].unsqueeze(2).to_broadcast([P, CHUNK, SIDES, HALF]),
-                    in1=gains[:, :, 1, mine].unsqueeze(1).to_broadcast([P, CHUNK, SIDES, HALF]),
-                    op=ALU.mult,
-                )
-            tables[c] = table
+            tables[j] = table
 
         transposed = {}
 
@@ -200,8 +197,7 @@ def tile_qwen3nextattentionforengine_pa_t_kernel(
 
         def multiply(j):
             heads, rstd = projected.pop(j)
-            first = (j % PAIRS_IN_CHUNK) * PAIR
-            table = tables[j // PAIRS_IN_CHUNK]
+            table = tables.pop(j)
             prod = prod_pool.tile([P, SIDES, PAIR, HEADS, 2, D], F32, name="prod")
             for t in range(PAIR):
                 for s in range(SIDES):
@@ -211,7 +207,7 @@ def tile_qwen3nextattentionforengine_pa_t_kernel(
                             out=prod[:, s, t, h, :, :],
                             in0=heads[:, g, :].unsqueeze(1).to_broadcast([P, 2, D]),
                             scalar=rstd[:, g : g + 1],
-                            in1=table[:, first + t, s, :, :],
+                            in1=table[:, t, s, :].rearrange("p (c d) -> p c d", c=2),
                             op0=ALU.mult,
                             op1=ALU.mult,
                         )
@@ -233,15 +229,14 @@ def tile_qwen3nextattentionforengine_pa_t_kernel(
                     in_=res[:, s].rearrange("p i h a d -> p i (h a d)"),
                 )
 
-        build_tables(0)
         for i in range(-4, PAIRS):
             if i + 4 < PAIRS:
                 if (i + 4) % PAIRS_IN_CHUNK == 0:
                     c = (i + 4) // PAIRS_IN_CHUNK
                     if c + 2 < CHUNKS:
                         load_x(c + 2, 1)
-                    if c + 1 < CHUNKS:
-                        build_tables(c + 1)
+                        load_angles(c + 2)
+                build_table(i + 4)
                 transpose(i + 4)
             if 0 <= i + 2 < PAIRS:
                 project_and_measure(i + 2)

@@ -31,6 +31,9 @@ CHUNK = 8
 PAIRS = TILES // PAIR
 PAIRS_IN_CHUNK = CHUNK // PAIR
 CHUNKS = TILES // CHUNK
+STEP = 2
+STEPS = PAIRS // STEP
+STEP_TILES = STEP * PAIR
 GROUPS = PAIR * SIDES * HEADS
 
 FLOPS = 2 * TOKENS * K * N_OUT
@@ -62,11 +65,11 @@ def tile_qwen3nextattentionforengine_pa_t_kernel(
     with ExitStack() as pools:
         const = pools.enter_context(tc.tile_pool(name="const", bufs=1))
         x_pool = pools.enter_context(tc.tile_pool(name="x_pool", bufs=3))
-        table_pool = pools.enter_context(tc.tile_pool(name="table_pool", bufs=4))
-        quant_pool = pools.enter_context(tc.tile_pool(name="quant_pool", bufs=3))
+        table_pool = pools.enter_context(tc.tile_pool(name="table_pool", bufs=2))
+        quant_pool = pools.enter_context(tc.tile_pool(name="quant_pool", bufs=4))
         stat_pool = pools.enter_context(tc.tile_pool(name="stat_pool", bufs=4))
-        prod_pool = pools.enter_context(tc.tile_pool(name="prod_pool", bufs=3))
-        res_pool = pools.enter_context(tc.tile_pool(name="res_pool", bufs=3))
+        prod_pool = pools.enter_context(tc.tile_pool(name="prod_pool", bufs=4))
+        res_pool = pools.enter_context(tc.tile_pool(name="res_pool", bufs=4))
         xt_psum = pools.enter_context(tc.psum_pool(name="xt_psum", bufs=3))
         v_psum = pools.enter_context(tc.psum_pool(name="v_psum", bufs=5))
         pools.enter_context(tc.manual_schedule())
@@ -83,9 +86,6 @@ def tile_qwen3nextattentionforengine_pa_t_kernel(
                 )
             x_chunks[c] = x_sb
 
-        gains = const.tile([P, SIDES, 2, D], BF16, name="gains")
-        nc.scalar.dma_start(out=gains[:, 0, 0, :], in_=q_norm_w.partition_broadcast(P))
-        nc.scalar.dma_start(out=gains[:, 1, 0, :], in_=k_norm_w.partition_broadcast(P))
         angles = const.tile([P, TILES, 2, D], BF16, name="angles")
 
         def load_angles(c):
@@ -94,7 +94,6 @@ def tile_qwen3nextattentionforengine_pa_t_kernel(
             nc.sync.dma_start(out=angles[:, tiles, 1, 0:HALF], in_=sin_view[:, tiles, HALF:D])
             nc.sync.dma_start(out=angles[:, tiles, 1, HALF:D], in_=sin_view[:, tiles, 0:HALF])
 
-        load_angles(0)
         load_x(0, 2)
 
         ident = const.tile([P, P], F32, name="ident")
@@ -103,13 +102,19 @@ def tile_qwen3nextattentionforengine_pa_t_kernel(
         nc.vector.memset(eps[:], EPS)
 
         w_words = const.tile([P, 2 * N_OUT], U8, name="w_words", align_bytes=64)
-        w_plane = const.tile([P, N_OUT], U8, name="w_plane", align_bytes=64)
-        nc.vector.memset(w_plane[:].bitcast(I32), 0)
         for s, words in enumerate((Wq_query_words, Wk_words)):
             nc.sync.dma_start(
                 out=w_words[:, s * 2 * N_SIDE : (s + 1) * 2 * N_SIDE].bitcast(I32),
                 in_=words.rearrange("g p n -> (g p) n").bitcast(I32),
             )
+
+        gains = const.tile([P, SIDES, 2, D], BF16, name="gains")
+        nc.scalar.dma_start(out=gains[:, 0, 0, :], in_=q_norm_w.partition_broadcast(P))
+        nc.scalar.dma_start(out=gains[:, 1, 0, :], in_=k_norm_w.partition_broadcast(P))
+        load_angles(0)
+
+        w_plane = const.tile([P, N_OUT], U8, name="w_plane", align_bytes=64)
+        nc.vector.memset(w_plane[:].bitcast(I32), 0)
         for s, scales in enumerate((Wq_query_scales, Wk_scales)):
             rows = scales.rearrange("g q n -> (g q) n")
             for quad in range(4):
@@ -126,18 +131,21 @@ def tile_qwen3nextattentionforengine_pa_t_kernel(
 
         tables = {}
 
-        def build_table(j):
-            table = table_pool.tile([P, PAIR, SIDES, 2 * D], F32, name="table")
-            nc.gpsimd.tensor_tensor(
+        def build_table(engine, q):
+            table = table_pool.tile([P, STEP_TILES, SIDES, 2 * D], F32, name="table")
+            engine.tensor_tensor(
                 out=table[:],
-                in0=angles[:, j * PAIR : (j + 1) * PAIR, :, :]
-                .rearrange("p t c d -> p t (c d)")
+                in0=angles[:, q * STEP_TILES : (q + 1) * STEP_TILES, :, :]
+                .rearrange("p i c d -> p i (c d)")
                 .unsqueeze(2)
-                .to_broadcast([P, PAIR, SIDES, 2 * D]),
-                in1=gains[:].rearrange("p s c d -> p s (c d)").unsqueeze(1).to_broadcast([P, PAIR, SIDES, 2 * D]),
+                .to_broadcast([P, STEP_TILES, SIDES, 2 * D]),
+                in1=gains[:]
+                .rearrange("p s c d -> p s (c d)")
+                .unsqueeze(1)
+                .to_broadcast([P, STEP_TILES, SIDES, 2 * D]),
                 op=ALU.mult,
             )
-            tables[j] = table
+            tables[q] = table
 
         transposed = {}
 
@@ -166,7 +174,7 @@ def tile_qwen3nextattentionforengine_pa_t_kernel(
 
         projected = {}
 
-        def project_and_measure(j):
+        def project(j):
             codes, plane = quantised.pop(j)
             v = v_psum.tile([P, PAIR, N_OUT], F32, name="v")
             for t in range(PAIR):
@@ -180,7 +188,12 @@ def tile_qwen3nextattentionforengine_pa_t_kernel(
                     start=True,
                     stop=True,
                 )
-            heads = v[:].rearrange("p t (g d) -> p (t g) d", d=D)
+            projected[j] = v[:].rearrange("p t (g d) -> p (t g) d", d=D)
+
+        measured = {}
+
+        def measure(j):
+            heads = projected[j]
             sumsq = stat_pool.tile([P, GROUPS], F32, name="sumsq")
             for g in range(GROUPS):
                 squares = stat_pool.tile([P, D], F32, name="squares")
@@ -191,13 +204,15 @@ def tile_qwen3nextattentionforengine_pa_t_kernel(
             nc.scalar.activation(
                 out=rstd[:], in_=sumsq[:], func=ACT.Abs_reciprocal_sqrt, bias=eps[:, 0:1], scale=1.0 / D
             )
-            projected[j] = (heads, rstd)
+            measured[j] = rstd
 
         products = {}
 
         def multiply(j):
-            heads, rstd = projected.pop(j)
-            table = tables.pop(j)
+            heads = projected.pop(j)
+            rstd = measured.pop(j)
+            table = tables[j // STEP]
+            first = (j % STEP) * PAIR
             prod = prod_pool.tile([P, SIDES, PAIR, HEADS, 2, D], F32, name="prod")
             for t in range(PAIR):
                 for s in range(SIDES):
@@ -207,7 +222,7 @@ def tile_qwen3nextattentionforengine_pa_t_kernel(
                             out=prod[:, s, t, h, :, :],
                             in0=heads[:, g, :].unsqueeze(1).to_broadcast([P, 2, D]),
                             scalar=rstd[:, g : g + 1],
-                            in1=table[:, t, s, :].rearrange("p (c d) -> p c d", c=2),
+                            in1=table[:, first + t, s, :].rearrange("p (c d) -> p c d", c=2),
                             op0=ALU.mult,
                             op1=ALU.mult,
                         )
@@ -229,20 +244,24 @@ def tile_qwen3nextattentionforengine_pa_t_kernel(
                     in_=res[:, s].rearrange("p i h a d -> p i (h a d)"),
                 )
 
-        for i in range(-4, PAIRS):
-            if i + 4 < PAIRS:
-                if (i + 4) % PAIRS_IN_CHUNK == 0:
-                    c = (i + 4) // PAIRS_IN_CHUNK
-                    if c + 2 < CHUNKS:
-                        load_x(c + 2, 1)
-                        load_angles(c + 2)
-                build_table(i + 4)
-                transpose(i + 4)
-            if 0 <= i + 2 < PAIRS:
-                project_and_measure(i + 2)
-            if i >= 0:
-                multiply(i)
-            if 0 <= i + 3 < PAIRS:
-                quantise(i + 3)
-            if i >= 0:
-                add_and_store(i)
+        def pairs_of(q):
+            return range(q * STEP, (q + 1) * STEP) if 0 <= q < STEPS else ()
+
+        for q in range(-2, STEPS):
+            for j in pairs_of(q + 1):
+                project(j)
+            for j in pairs_of(q + 2):
+                if j % PAIRS_IN_CHUNK == 0 and j // PAIRS_IN_CHUNK + 2 < CHUNKS:
+                    load_x(j // PAIRS_IN_CHUNK + 2, 1)
+                    load_angles(j // PAIRS_IN_CHUNK + 2)
+                transpose(j)
+            for j in pairs_of(q + 1):
+                measure(j)
+            for j in pairs_of(q):
+                multiply(j)
+            for j in pairs_of(q + 2):
+                quantise(j)
+            for j in pairs_of(q):
+                add_and_store(j)
+            if q + 2 < STEPS:
+                build_table(nc.vector if q < 0 else nc.gpsimd, q + 2)

@@ -26,15 +26,15 @@ N_SIDE = HEADS * D
 N_OUT = SIDES * N_SIDE
 EPS = 1e-6
 
-PAIR = 2
+BANK_TILES = 2
+STEP_TILES = 4
+STEP_BANKS = STEP_TILES // BANK_TILES
+STEPS = TILES // STEP_TILES
+GROUPS = STEP_TILES * SIDES * HEADS
+BANK_GROUPS = GROUPS // STEP_BANKS
 CHUNK = 8
-PAIRS = TILES // PAIR
-PAIRS_IN_CHUNK = CHUNK // PAIR
 CHUNKS = TILES // CHUNK
-STEP = 2
-STEPS = PAIRS // STEP
-STEP_TILES = STEP * PAIR
-GROUPS = PAIR * SIDES * HEADS
+CHUNK_STEPS = CHUNK // STEP_TILES
 
 FLOPS = 2 * TOKENS * K * N_OUT
 
@@ -66,24 +66,22 @@ def tile_qwen3nextattentionforengine_pa_t_kernel(
         const = pools.enter_context(tc.tile_pool(name="const", bufs=1))
         x_pool = pools.enter_context(tc.tile_pool(name="x_pool", bufs=3))
         table_pool = pools.enter_context(tc.tile_pool(name="table_pool", bufs=2))
-        quant_pool = pools.enter_context(tc.tile_pool(name="quant_pool", bufs=4))
-        stat_pool = pools.enter_context(tc.tile_pool(name="stat_pool", bufs=4))
-        prod_pool = pools.enter_context(tc.tile_pool(name="prod_pool", bufs=4))
-        res_pool = pools.enter_context(tc.tile_pool(name="res_pool", bufs=4))
+        quant_pool = pools.enter_context(tc.tile_pool(name="quant_pool", bufs=3))
+        stat_pool = pools.enter_context(tc.tile_pool(name="stat_pool", bufs=3))
+        prod_pool = pools.enter_context(tc.tile_pool(name="prod_pool", bufs=2))
+        res_pool = pools.enter_context(tc.tile_pool(name="res_pool", bufs=3))
         xt_psum = pools.enter_context(tc.psum_pool(name="xt_psum", bufs=3))
         v_psum = pools.enter_context(tc.psum_pool(name="v_psum", bufs=5))
         pools.enter_context(tc.manual_schedule())
 
         x_chunks = {}
 
-        def load_x(c, pieces):
+        def load_x(c, queues):
             x_sb = x_pool.tile([P, CHUNK, K], BF16, name="x_sb")
-            step = CHUNK // pieces
-            for first in range(0, CHUNK, step):
-                nc.sync.dma_start(
-                    out=x_sb[:, first : first + step, :],
-                    in_=x_view[:, c * CHUNK + first : c * CHUNK + first + step, :],
-                )
+            size = CHUNK // len(queues)
+            for piece, queue in enumerate(queues):
+                tiles = slice(piece * size, (piece + 1) * size)
+                queue.dma_start(out=x_sb[:, tiles, :], in_=x_view[:, c * CHUNK : (c + 1) * CHUNK, :][:, tiles, :])
             x_chunks[c] = x_sb
 
         angles = const.tile([P, TILES, 2, D], BF16, name="angles")
@@ -94,10 +92,14 @@ def tile_qwen3nextattentionforengine_pa_t_kernel(
             nc.sync.dma_start(out=angles[:, tiles, 1, 0:HALF], in_=sin_view[:, tiles, HALF:D])
             nc.sync.dma_start(out=angles[:, tiles, 1, HALF:D], in_=sin_view[:, tiles, 0:HALF])
 
-        load_x(0, 2)
-
         ident = const.tile([P, P], F32, name="ident")
         make_identity(nc, ident[:])
+        load_x(0, (nc.sync, nc.gpsimd))
+        gains = const.tile([P, SIDES, 2, D], BF16, name="gains")
+        nc.scalar.dma_start(out=gains[:, 0, 0, :], in_=q_norm_w.partition_broadcast(P))
+        nc.scalar.dma_start(out=gains[:, 1, 0, :], in_=k_norm_w.partition_broadcast(P))
+        load_angles(0)
+
         eps = const.tile([P, 1], F32, name="eps")
         nc.vector.memset(eps[:], EPS)
 
@@ -107,12 +109,6 @@ def tile_qwen3nextattentionforengine_pa_t_kernel(
                 out=w_words[:, s * 2 * N_SIDE : (s + 1) * 2 * N_SIDE].bitcast(I32),
                 in_=words.rearrange("g p n -> (g p) n").bitcast(I32),
             )
-
-        gains = const.tile([P, SIDES, 2, D], BF16, name="gains")
-        nc.scalar.dma_start(out=gains[:, 0, 0, :], in_=q_norm_w.partition_broadcast(P))
-        nc.scalar.dma_start(out=gains[:, 1, 0, :], in_=k_norm_w.partition_broadcast(P))
-        load_angles(0)
-
         w_plane = const.tile([P, N_OUT], U8, name="w_plane", align_bytes=64)
         nc.vector.memset(w_plane[:].bitcast(I32), 0)
         for s, scales in enumerate((Wq_query_scales, Wk_scales)):
@@ -122,8 +118,7 @@ def tile_qwen3nextattentionforengine_pa_t_kernel(
                     out=w_plane[32 * quad : 32 * quad + 4, s * N_SIDE : (s + 1) * N_SIDE].bitcast(I32),
                     in_=rows[4 * quad : 4 * quad + 4, :].bitcast(I32),
                 )
-
-        load_x(1, 1)
+        load_x(1, (nc.sync,))
         load_angles(1)
 
         nc.vector.tensor_copy(out=gains[:, :, 1, 0:HALF], in_=gains[:, :, 0, 0:HALF])
@@ -132,105 +127,111 @@ def tile_qwen3nextattentionforengine_pa_t_kernel(
         tables = {}
 
         def build_table(engine, q):
-            table = table_pool.tile([P, STEP_TILES, SIDES, 2 * D], F32, name="table")
+            table = table_pool.tile([P, STEP_TILES, SIDES, 2, D], F32, name="table")
+            shape = [P, STEP_TILES, SIDES, 2 * D]
             engine.tensor_tensor(
-                out=table[:],
+                out=table[:].rearrange("p i s c d -> p i s (c d)"),
                 in0=angles[:, q * STEP_TILES : (q + 1) * STEP_TILES, :, :]
                 .rearrange("p i c d -> p i (c d)")
                 .unsqueeze(2)
-                .to_broadcast([P, STEP_TILES, SIDES, 2 * D]),
-                in1=gains[:]
-                .rearrange("p s c d -> p s (c d)")
-                .unsqueeze(1)
-                .to_broadcast([P, STEP_TILES, SIDES, 2 * D]),
+                .to_broadcast(shape),
+                in1=gains[:].rearrange("p s c d -> p s (c d)").unsqueeze(1).to_broadcast(shape),
                 op=ALU.mult,
             )
             tables[q] = table
 
         transposed = {}
 
-        def transpose(j):
-            x_sb = x_chunks[j // PAIRS_IN_CHUNK]
-            xt = xt_psum.tile([P, PAIR, 2, P], F32, name="xt")
-            for t in range(PAIR):
-                words = x_sb[:, (j % PAIRS_IN_CHUNK) * PAIR + t, :].bitcast(F32)
-                for u in range(2):
-                    nc.tensor.transpose(xt[:, t, u, :], words[:, u : K // 2 : 2], ident[:])
-            grouped = quant_pool.tile([P, PAIR * P * PACK], BF16, name="grouped", align_bytes=64)
-            nc.scalar.copy(
-                out=grouped[:].bitcast(F32).rearrange("p (t r u) -> p t r u", t=PAIR, u=2),
-                in_=xt[:].rearrange("p t u r -> p t r u"),
-            )
-            transposed[j] = grouped
+        def transpose(q):
+            x_sb = x_chunks[q // CHUNK_STEPS]
+            first = (q % CHUNK_STEPS) * STEP_TILES
+            grouped = quant_pool.tile([P, STEP_BANKS, BANK_TILES * P * PACK], BF16, name="grouped", align_bytes=64)
+            for b in range(STEP_BANKS):
+                xt = xt_psum.tile([P, BANK_TILES, 2, P], F32, name="xt")
+                for t in range(BANK_TILES):
+                    words = x_sb[:, first + b * BANK_TILES + t, :].bitcast(F32)
+                    for u in range(2):
+                        nc.tensor.transpose(xt[:, t, u, :], words[:, u : K // 2 : 2], ident[:])
+                nc.scalar.copy(
+                    out=grouped[:, b, :].bitcast(F32).rearrange("p (t r u) -> p t r u", t=BANK_TILES, u=2),
+                    in_=xt[:].rearrange("p t u r -> p t r u"),
+                )
+            transposed[q] = grouped
 
         quantised = {}
 
-        def quantise(j):
-            grouped = transposed.pop(j)
-            codes = quant_pool.tile([P, PAIR * P], U32, name="codes", align_bytes=64)
-            plane = quant_pool.tile([P, PAIR * P], U8, name="plane", align_bytes=64)
-            nc.vector.quantize_mx(out=codes[:].bitcast(FP8X4), scales=plane[:], in_=grouped[:])
-            quantised[j] = (codes, plane)
+        def quantise(q):
+            grouped = transposed.pop(q)
+            codes = quant_pool.tile([P, STEP_TILES * P], U32, name="codes", align_bytes=64)
+            plane = quant_pool.tile([P, STEP_TILES * P], U8, name="plane", align_bytes=64)
+            nc.vector.quantize_mx(
+                out=codes[:].bitcast(FP8X4), scales=plane[:], in_=grouped[:].rearrange("p b n -> p (b n)")
+            )
+            quantised[q] = (codes, plane)
 
         projected = {}
 
-        def project(j):
-            codes, plane = quantised.pop(j)
-            v = v_psum.tile([P, PAIR, N_OUT], F32, name="v")
-            for t in range(PAIR):
-                tokens = slice(t * P, (t + 1) * P)
-                nc.tensor.matmul_mx(
-                    out=v[:, t, :],
-                    lhsT=codes[:, tokens].bitcast(FP8X4),
-                    lhsT_scale=plane[:, tokens],
-                    rhs=w_words[:].bitcast(FP4X4),
-                    rhs_scale=w_plane[:],
-                    start=True,
-                    stop=True,
-                )
-            projected[j] = v[:].rearrange("p t (g d) -> p (t g) d", d=D)
+        def project(q):
+            codes, plane = quantised.pop(q)
+            heads = []
+            for b in range(STEP_BANKS):
+                v = v_psum.tile([P, BANK_TILES, N_OUT], F32, name="v")
+                for t in range(BANK_TILES):
+                    tokens = slice((b * BANK_TILES + t) * P, (b * BANK_TILES + t + 1) * P)
+                    nc.tensor.matmul_mx(
+                        out=v[:, t, :],
+                        lhsT=codes[:, tokens].bitcast(FP8X4),
+                        lhsT_scale=plane[:, tokens],
+                        rhs=w_words[:].bitcast(FP4X4),
+                        rhs_scale=w_plane[:],
+                        start=True,
+                        stop=True,
+                    )
+                    heads.extend(v[:, t, n : n + D] for n in range(0, N_OUT, D))
+            projected[q] = heads
 
         measured = {}
 
-        def measure(j):
-            heads = projected[j]
+        def measure(q):
+            heads = projected[q]
             sumsq = stat_pool.tile([P, GROUPS], F32, name="sumsq")
-            for g in range(GROUPS):
-                squares = stat_pool.tile([P, D], F32, name="squares")
-                nc.scalar.activation(
-                    out=squares[:], in_=heads[:, g, :], func=ACT.Square, accum_out=sumsq[:, g : g + 1]
-                )
             rstd = stat_pool.tile([P, GROUPS], F32, name="rstd")
-            nc.scalar.activation(
-                out=rstd[:], in_=sumsq[:], func=ACT.Abs_reciprocal_sqrt, bias=eps[:, 0:1], scale=1.0 / D
-            )
-            measured[j] = rstd
+            for b in range(STEP_BANKS):
+                bank = slice(b * BANK_GROUPS, (b + 1) * BANK_GROUPS)
+                for g in range(b * BANK_GROUPS, (b + 1) * BANK_GROUPS):
+                    squares = stat_pool.tile([P, D], F32, name="squares")
+                    nc.scalar.activation(
+                        out=squares[:], in_=heads[g], func=ACT.Square, accum_out=sumsq[:, g : g + 1]
+                    )
+                nc.scalar.activation(
+                    out=rstd[:, bank], in_=sumsq[:, bank], func=ACT.Abs_reciprocal_sqrt, bias=eps[:, 0:1], scale=1.0 / D
+                )
+            measured[q] = rstd
 
         products = {}
 
-        def multiply(j):
-            heads = projected.pop(j)
-            rstd = measured.pop(j)
-            table = tables[j // STEP]
-            first = (j % STEP) * PAIR
-            prod = prod_pool.tile([P, SIDES, PAIR, HEADS, 2, D], F32, name="prod")
-            for t in range(PAIR):
+        def multiply(q):
+            heads = projected.pop(q)
+            rstd = measured.pop(q)
+            table = tables.pop(q)
+            prod = prod_pool.tile([P, SIDES, STEP_TILES, HEADS, 2, D], F32, name="prod")
+            for i in range(STEP_TILES):
                 for s in range(SIDES):
                     for h in range(HEADS):
-                        g = (t * SIDES + s) * HEADS + h
+                        g = (i * SIDES + s) * HEADS + h
                         nc.vector.scalar_tensor_tensor(
-                            out=prod[:, s, t, h, :, :],
-                            in0=heads[:, g, :].unsqueeze(1).to_broadcast([P, 2, D]),
+                            out=prod[:, s, i, h, :, :],
+                            in0=heads[g].unsqueeze(1).to_broadcast([P, 2, D]),
                             scalar=rstd[:, g : g + 1],
-                            in1=table[:, first + t, s, :].rearrange("p (c d) -> p c d", c=2),
+                            in1=table[:, i, s, :, :],
                             op0=ALU.mult,
                             op1=ALU.mult,
                         )
-            products[j] = prod
+            products[q] = prod
 
-        def add_and_store(j):
-            prod = products.pop(j)
-            res = res_pool.tile([P, SIDES, PAIR, HEADS, 2, HALF], F32, name="res")
+        def add_and_store(q):
+            prod = products.pop(q)
+            res = res_pool.tile([P, SIDES, STEP_TILES, HEADS, 2, HALF], F32, name="res")
             for a in range(2):
                 nc.vector.tensor_tensor(
                     out=res[:, :, :, :, a, :],
@@ -240,28 +241,27 @@ def tile_qwen3nextattentionforengine_pa_t_kernel(
                 )
             for s in range(SIDES):
                 nc.sync.dma_start(
-                    out=out_views[s][:, j * PAIR : (j + 1) * PAIR, :],
+                    out=out_views[s][:, q * STEP_TILES : (q + 1) * STEP_TILES, :],
                     in_=res[:, s].rearrange("p i h a d -> p i (h a d)"),
                 )
 
-        def pairs_of(q):
-            return range(q * STEP, (q + 1) * STEP) if 0 <= q < STEPS else ()
-
-        for q in range(-2, STEPS):
-            for j in pairs_of(q + 1):
-                project(j)
-            for j in pairs_of(q + 2):
-                if j % PAIRS_IN_CHUNK == 0 and j // PAIRS_IN_CHUNK + 2 < CHUNKS:
-                    load_x(j // PAIRS_IN_CHUNK + 2, 1)
-                    load_angles(j // PAIRS_IN_CHUNK + 2)
-                transpose(j)
-            for j in pairs_of(q + 1):
-                measure(j)
-            for j in pairs_of(q):
-                multiply(j)
-            for j in pairs_of(q + 2):
-                quantise(j)
-            for j in pairs_of(q):
-                add_and_store(j)
-            if q + 2 < STEPS:
-                build_table(nc.vector if q < 0 else nc.gpsimd, q + 2)
+        build_table(nc.vector, 0)
+        build_table(nc.vector, 1)
+        for q in range(-3, STEPS):
+            if 0 <= q + 1 < STEPS:
+                project(q + 1)
+                measure(q + 1)
+            if q + 3 < STEPS:
+                c = (q + 3) // CHUNK_STEPS
+                if (q + 3) % CHUNK_STEPS == 0 and c + 2 < CHUNKS:
+                    load_x(c + 2, (nc.sync,))
+                    load_angles(c + 2)
+                transpose(q + 3)
+            if q >= 0:
+                multiply(q)
+            if 0 <= q + 2 < STEPS:
+                quantise(q + 2)
+            if q >= 0:
+                add_and_store(q)
+                if q + 2 < STEPS:
+                    build_table(nc.gpsimd, q + 2)

@@ -35,6 +35,8 @@ BANK_GROUPS = GROUPS // STEP_BANKS
 CHUNK = 8
 CHUNKS = TILES // CHUNK
 CHUNK_STEPS = CHUNK // STEP_TILES
+TABLE_LEAD = 4
+GPSIMD_TABLE_TILES = 1
 
 FLOPS = 2 * TOKENS * K * N_OUT
 
@@ -65,13 +67,13 @@ def tile_qwen3nextattentionforengine_pa_t_kernel(
     with ExitStack() as pools:
         const = pools.enter_context(tc.tile_pool(name="const", bufs=1))
         x_pool = pools.enter_context(tc.tile_pool(name="x_pool", bufs=3))
-        table_pool = pools.enter_context(tc.tile_pool(name="table_pool", bufs=2))
         quant_pool = pools.enter_context(tc.tile_pool(name="quant_pool", bufs=3))
         stat_pool = pools.enter_context(tc.tile_pool(name="stat_pool", bufs=3))
-        prod_pool = pools.enter_context(tc.tile_pool(name="prod_pool", bufs=2))
+        prod_pool = pools.enter_context(tc.tile_pool(name="prod_pool", bufs=3))
         res_pool = pools.enter_context(tc.tile_pool(name="res_pool", bufs=3))
         xt_psum = pools.enter_context(tc.psum_pool(name="xt_psum", bufs=3))
-        v_psum = pools.enter_context(tc.psum_pool(name="v_psum", bufs=5))
+        v_psum = pools.enter_context(tc.psum_pool(name="v_psum", bufs=4))
+        gain_psum = pools.enter_context(tc.psum_pool(name="gain_psum", bufs=1))
         pools.enter_context(tc.manual_schedule())
 
         x_chunks = {}
@@ -121,24 +123,37 @@ def tile_qwen3nextattentionforengine_pa_t_kernel(
         load_x(1, (nc.sync,))
         load_angles(1)
 
+        ident_bf = const.tile([P, P], BF16, name="ident_bf")
+        nc.vector.tensor_copy(out=ident_bf[:], in_=ident[:])
         nc.vector.tensor_copy(out=gains[:, :, 1, 0:HALF], in_=gains[:, :, 0, 0:HALF])
         nc.vector.tensor_scalar_mul(out=gains[:, :, 1, HALF:D], in0=gains[:, :, 0, HALF:D], scalar1=-1.0)
 
-        tables = {}
+        gains_ps = gain_psum.tile([P, SIDES, 2 * D], F32, name="gains_ps")
 
-        def build_table(engine, q):
-            table = table_pool.tile([P, STEP_TILES, SIDES, 2, D], F32, name="table")
-            shape = [P, STEP_TILES, SIDES, 2 * D]
+        def gains_to_psum():
+            nc.tensor.matmul(
+                out=gains_ps[:].rearrange("p s n -> p (s n)"),
+                lhsT=ident_bf[:],
+                rhs=gains[:].rearrange("p s c d -> p (s c d)"),
+                start=True,
+                stop=True,
+            )
+
+        tables = const.tile([P, TILES, SIDES, 2, D], F32, name="tables")
+
+        def build_table(on_vector, first, count):
+            shape = [P, count, SIDES, 2 * D]
+            engine = nc.vector if on_vector else nc.gpsimd
+            factors = gains_ps[:] if on_vector else gains[:].rearrange("p s c d -> p s (c d)")
             engine.tensor_tensor(
-                out=table[:].rearrange("p i s c d -> p i s (c d)"),
-                in0=angles[:, q * STEP_TILES : (q + 1) * STEP_TILES, :, :]
+                out=tables[:, first : first + count].rearrange("p i s c d -> p i s (c d)"),
+                in0=angles[:, first : first + count, :, :]
                 .rearrange("p i c d -> p i (c d)")
                 .unsqueeze(2)
                 .to_broadcast(shape),
-                in1=gains[:].rearrange("p s c d -> p s (c d)").unsqueeze(1).to_broadcast(shape),
+                in1=factors.unsqueeze(1).to_broadcast(shape),
                 op=ALU.mult,
             )
-            tables[q] = table
 
         transposed = {}
 
@@ -210,15 +225,17 @@ def tile_qwen3nextattentionforengine_pa_t_kernel(
 
         products = {}
 
-        def multiply(q):
+        def multiply(q, before_last):
             heads = projected.pop(q)
             rstd = measured.pop(q)
-            table = tables.pop(q)
+            table = tables[:, q * STEP_TILES : (q + 1) * STEP_TILES]
             prod = prod_pool.tile([P, SIDES, STEP_TILES, HEADS, 2, D], F32, name="prod")
             for i in range(STEP_TILES):
                 for s in range(SIDES):
                     for h in range(HEADS):
                         g = (i * SIDES + s) * HEADS + h
+                        if g == GROUPS - 1:
+                            before_last()
                         nc.vector.scalar_tensor_tensor(
                             out=prod[:, s, i, h, :, :],
                             in0=heads[g].unsqueeze(1).to_broadcast([P, 2, D]),
@@ -229,11 +246,11 @@ def tile_qwen3nextattentionforengine_pa_t_kernel(
                         )
             products[q] = prod
 
-        def add_and_store(q):
+        def add_and_store(engine, q):
             prod = products.pop(q)
             res = res_pool.tile([P, SIDES, STEP_TILES, HEADS, 2, HALF], F32, name="res")
             for a in range(2):
-                nc.vector.tensor_tensor(
+                engine.tensor_tensor(
                     out=res[:, :, :, :, a, :],
                     in0=prod[:, :, :, :, 0, a * HALF : (a + 1) * HALF],
                     in1=prod[:, :, :, :, 1, (1 - a) * HALF : (2 - a) * HALF],
@@ -245,8 +262,10 @@ def tile_qwen3nextattentionforengine_pa_t_kernel(
                     in_=res[:, s].rearrange("p i h a d -> p i (h a d)"),
                 )
 
-        build_table(nc.vector, 0)
-        build_table(nc.vector, 1)
+        def quantise_next(q):
+            if 0 <= q + 2 < STEPS:
+                quantise(q + 2)
+
         for q in range(-3, STEPS):
             if 0 <= q + 1 < STEPS:
                 project(q + 1)
@@ -257,11 +276,18 @@ def tile_qwen3nextattentionforengine_pa_t_kernel(
                     load_x(c + 2, (nc.sync,))
                     load_angles(c + 2)
                 transpose(q + 3)
+            if q == -3:
+                gains_to_psum()
+                build_table(True, 0, STEP_TILES)
+                for ahead in range(1, TABLE_LEAD):
+                    build_table(False, ahead * STEP_TILES, STEP_TILES)
             if q >= 0:
-                multiply(q)
-            if 0 <= q + 2 < STEPS:
-                quantise(q + 2)
-            if q >= 0:
-                add_and_store(q)
-                if q + 2 < STEPS:
-                    build_table(nc.gpsimd, q + 2)
+                multiply(q, lambda: quantise_next(q))
+                add_and_store(nc.gpsimd if q + 1 < STEPS else nc.vector, q)
+                if q + TABLE_LEAD < STEPS:
+                    first = (q + TABLE_LEAD) * STEP_TILES
+                    build_table(True, first, STEP_TILES - GPSIMD_TABLE_TILES)
+                    if GPSIMD_TABLE_TILES:
+                        build_table(False, first + STEP_TILES - GPSIMD_TABLE_TILES, GPSIMD_TABLE_TILES)
+            else:
+                quantise_next(q)

@@ -225,7 +225,7 @@ def tile_qwen3nextattentionforengine_pa_t_kernel(
 
         products = {}
 
-        def multiply(q, before_last):
+        def multiply(q):
             heads = projected.pop(q)
             rstd = measured.pop(q)
             table = tables[:, q * STEP_TILES : (q + 1) * STEP_TILES]
@@ -234,8 +234,6 @@ def tile_qwen3nextattentionforengine_pa_t_kernel(
                 for s in range(SIDES):
                     for h in range(HEADS):
                         g = (i * SIDES + s) * HEADS + h
-                        if g == GROUPS - 1:
-                            before_last()
                         nc.vector.scalar_tensor_tensor(
                             out=prod[:, s, i, h, :, :],
                             in0=heads[g].unsqueeze(1).to_broadcast([P, 2, D]),
@@ -249,13 +247,13 @@ def tile_qwen3nextattentionforengine_pa_t_kernel(
         def add_and_store(engine, q):
             prod = products.pop(q)
             res = res_pool.tile([P, SIDES, STEP_TILES, HEADS, 2, HALF], F32, name="res")
-            for a in range(2):
-                engine.tensor_tensor(
-                    out=res[:, :, :, :, a, :],
-                    in0=prod[:, :, :, :, 0, a * HALF : (a + 1) * HALF],
-                    in1=prod[:, :, :, :, 1, (1 - a) * HALF : (2 - a) * HALF],
-                    op=ALU.add,
-                )
+            halves = prod[:].rearrange("p s i h c (a d) -> p (s i h) c a d", a=2)
+            engine.tensor_tensor(
+                out=res[:].rearrange("p s i h a d -> p (s i h) a d"),
+                in0=halves[:, :, 0, :, :],
+                in1=halves[:, :, 1, ::-1, :],
+                op=ALU.add,
+            )
             for s in range(SIDES):
                 nc.sync.dma_start(
                     out=out_views[s][:, q * STEP_TILES : (q + 1) * STEP_TILES, :],
@@ -282,7 +280,8 @@ def tile_qwen3nextattentionforengine_pa_t_kernel(
                 for ahead in range(1, TABLE_LEAD):
                     build_table(False, ahead * STEP_TILES, STEP_TILES)
             if q >= 0:
-                multiply(q, lambda: quantise_next(q))
+                multiply(q)
+                quantise_next(q)
                 add_and_store(nc.gpsimd if q + 1 < STEPS else nc.vector, q)
                 if q + TABLE_LEAD < STEPS:
                     first = (q + TABLE_LEAD) * STEP_TILES

@@ -139,12 +139,14 @@ def tile_qwen3nextattentionforengine_pa_t_kernel(
                 stop=True,
             )
 
+        gains_late = const.tile([P, SIDES, 2 * D], BF16, name="gains_late")
+
         tables = const.tile([P, TILES, SIDES, 2, D], F32, name="tables")
 
         def build_table(on_vector, first, count):
             shape = [P, count, SIDES, 2 * D]
             engine = nc.vector if on_vector else nc.gpsimd
-            factors = gains_ps[:] if on_vector else gains[:].rearrange("p s c d -> p s (c d)")
+            factors = gains_ps[:] if on_vector else gains_late[:]
             engine.tensor_tensor(
                 out=tables[:, first : first + count].rearrange("p i s c d -> p i s (c d)"),
                 in0=angles[:, first : first + count, :, :]
@@ -277,8 +279,7 @@ def tile_qwen3nextattentionforengine_pa_t_kernel(
             if q == -3:
                 gains_to_psum()
                 build_table(True, 0, STEP_TILES)
-                for ahead in range(1, TABLE_LEAD):
-                    build_table(False, ahead * STEP_TILES, STEP_TILES)
+                build_table(True, STEP_TILES, STEP_TILES)
             if q >= 0:
                 multiply(q)
                 quantise_next(q)
@@ -290,3 +291,8 @@ def tile_qwen3nextattentionforengine_pa_t_kernel(
                         build_table(False, first + STEP_TILES - GPSIMD_TABLE_TILES, GPSIMD_TABLE_TILES)
             else:
                 quantise_next(q)
+                if q == -2:
+                    build_table(True, 2 * STEP_TILES, STEP_TILES)
+                if q == -1:
+                    nc.vector.tensor_copy(out=gains_late[:], in_=gains[:].rearrange("p s c d -> p s (c d)"))
+                    build_table(False, 3 * STEP_TILES, STEP_TILES)

@@ -36,7 +36,7 @@ CHUNK = 8
 CHUNKS = TILES // CHUNK
 CHUNK_STEPS = CHUNK // STEP_TILES
 TABLE_LEAD = 4
-GPSIMD_TABLE_TILES = 1
+GPSIMD_COS_TILES = 2
 
 FLOPS = 2 * TOKENS * K * N_OUT
 
@@ -86,13 +86,12 @@ def tile_qwen3nextattentionforengine_pa_t_kernel(
                 queue.dma_start(out=x_sb[:, tiles, :], in_=x_view[:, c * CHUNK : (c + 1) * CHUNK, :][:, tiles, :])
             x_chunks[c] = x_sb
 
-        angles = const.tile([P, TILES, 2, D], BF16, name="angles")
+        angles = const.tile([P, 2, TILES, D], BF16, name="angles")
 
         def load_angles(c):
             tiles = slice(c * CHUNK, (c + 1) * CHUNK)
-            nc.sync.dma_start(out=angles[:, tiles, 0, :], in_=cos_view[:, tiles, :])
-            nc.sync.dma_start(out=angles[:, tiles, 1, 0:HALF], in_=sin_view[:, tiles, HALF:D])
-            nc.sync.dma_start(out=angles[:, tiles, 1, HALF:D], in_=sin_view[:, tiles, 0:HALF])
+            nc.sync.dma_start(out=angles[:, 0, tiles, :], in_=cos_view[:, tiles, :])
+            nc.sync.dma_start(out=angles[:, 1, tiles, :], in_=sin_view[:, tiles, :])
 
         ident = const.tile([P, P], F32, name="ident")
         make_identity(nc, ident[:])
@@ -143,19 +142,34 @@ def tile_qwen3nextattentionforengine_pa_t_kernel(
 
         tables = const.tile([P, TILES, SIDES, 2, D], F32, name="tables")
 
-        def build_table(on_vector, first, count):
-            shape = [P, count, SIDES, 2 * D]
+        def build_cos(on_vector, first, count):
+            shape = [P, count, SIDES, D]
             engine = nc.vector if on_vector else nc.gpsimd
             factors = gains_ps[:] if on_vector else gains_late[:]
             engine.tensor_tensor(
-                out=tables[:, first : first + count].rearrange("p i s c d -> p i s (c d)"),
-                in0=angles[:, first : first + count, :, :]
-                .rearrange("p i c d -> p i (c d)")
-                .unsqueeze(2)
-                .to_broadcast(shape),
-                in1=factors.unsqueeze(1).to_broadcast(shape),
+                out=tables[:, first : first + count, :, 0, :],
+                in0=angles[:, 0, first : first + count, :].unsqueeze(2).to_broadcast(shape),
+                in1=factors[:, :, 0:D].unsqueeze(1).to_broadcast(shape),
                 op=ALU.mult,
             )
+
+        def build_sin(on_vector, first, count):
+            shape = [P, count, SIDES, HALF]
+            engine = nc.vector if on_vector else nc.gpsimd
+            factors = gains_ps[:] if on_vector else gains_late[:]
+            for a in range(2):
+                engine.tensor_tensor(
+                    out=tables[:, first : first + count, :, 1, a * HALF : (a + 1) * HALF],
+                    in0=angles[:, 1, first : first + count, (1 - a) * HALF : (2 - a) * HALF]
+                    .unsqueeze(2)
+                    .to_broadcast(shape),
+                    in1=factors[:, :, D + a * HALF : D + (a + 1) * HALF].unsqueeze(1).to_broadcast(shape),
+                    op=ALU.mult,
+                )
+
+        def build_table(on_vector, q):
+            build_cos(on_vector, q * STEP_TILES, STEP_TILES)
+            build_sin(on_vector, q * STEP_TILES, STEP_TILES)
 
         transposed = {}
 
@@ -278,21 +292,21 @@ def tile_qwen3nextattentionforengine_pa_t_kernel(
                 transpose(q + 3)
             if q == -3:
                 gains_to_psum()
-                build_table(True, 0, STEP_TILES)
-                build_table(True, STEP_TILES, STEP_TILES)
+                build_table(True, 0)
+                build_table(True, 1)
             if q >= 0:
                 multiply(q)
                 quantise_next(q)
                 add_and_store(nc.gpsimd if q + 1 < STEPS else nc.vector, q)
                 if q + TABLE_LEAD < STEPS:
                     first = (q + TABLE_LEAD) * STEP_TILES
-                    build_table(True, first, STEP_TILES - GPSIMD_TABLE_TILES)
-                    if GPSIMD_TABLE_TILES:
-                        build_table(False, first + STEP_TILES - GPSIMD_TABLE_TILES, GPSIMD_TABLE_TILES)
+                    build_cos(True, first, STEP_TILES - GPSIMD_COS_TILES)
+                    build_sin(True, first, STEP_TILES)
+                    build_cos(False, first + STEP_TILES - GPSIMD_COS_TILES, GPSIMD_COS_TILES)
             else:
                 quantise_next(q)
                 if q == -2:
-                    build_table(True, 2 * STEP_TILES, STEP_TILES)
+                    build_table(True, 2)
                 if q == -1:
                     nc.vector.tensor_copy(out=gains_late[:], in_=gains[:].rearrange("p s c d -> p s (c d)"))
-                    build_table(False, 3 * STEP_TILES, STEP_TILES)
+                    build_table(False, 3)

@@ -35,7 +35,8 @@ BANK_GROUPS = GROUPS // STEP_BANKS
 CHUNK = 8
 CHUNKS = TILES // CHUNK
 CHUNK_STEPS = CHUNK // STEP_TILES
-TABLE_LEAD = 4
+TABLE_LEAD = 6
+VECTOR_HEAD_STEPS = 3
 GPSIMD_COS_TILES = 2
 
 FLOPS = 2 * TOKENS * K * N_OUT
@@ -119,8 +120,9 @@ def tile_qwen3nextattentionforengine_pa_t_kernel(
                     out=w_plane[32 * quad : 32 * quad + 4, s * N_SIDE : (s + 1) * N_SIDE].bitcast(I32),
                     in_=rows[4 * quad : 4 * quad + 4, :].bitcast(I32),
                 )
-        load_x(1, (nc.sync,))
         load_angles(1)
+        load_angles(2)
+        load_x(1, (nc.sync,))
 
         ident_bf = const.tile([P, P], BF16, name="ident_bf")
         nc.vector.tensor_copy(out=ident_bf[:], in_=ident[:])
@@ -138,14 +140,12 @@ def tile_qwen3nextattentionforengine_pa_t_kernel(
                 stop=True,
             )
 
-        gains_late = const.tile([P, SIDES, 2 * D], BF16, name="gains_late")
-
         tables = const.tile([P, TILES, SIDES, 2, D], F32, name="tables")
 
         def build_cos(on_vector, first, count):
             shape = [P, count, SIDES, D]
             engine = nc.vector if on_vector else nc.gpsimd
-            factors = gains_ps[:] if on_vector else gains_late[:]
+            factors = gains_ps[:] if on_vector else gains[:].rearrange("p s c d -> p s (c d)")
             engine.tensor_tensor(
                 out=tables[:, first : first + count, :, 0, :],
                 in0=angles[:, 0, first : first + count, :].unsqueeze(2).to_broadcast(shape),
@@ -156,7 +156,7 @@ def tile_qwen3nextattentionforengine_pa_t_kernel(
         def build_sin(on_vector, first, count):
             shape = [P, count, SIDES, HALF]
             engine = nc.vector if on_vector else nc.gpsimd
-            factors = gains_ps[:] if on_vector else gains_late[:]
+            factors = gains_ps[:] if on_vector else gains[:].rearrange("p s c d -> p s (c d)")
             for a in range(2):
                 engine.tensor_tensor(
                     out=tables[:, first : first + count, :, 1, a * HALF : (a + 1) * HALF],
@@ -288,12 +288,15 @@ def tile_qwen3nextattentionforengine_pa_t_kernel(
                 c = (q + 3) // CHUNK_STEPS
                 if (q + 3) % CHUNK_STEPS == 0 and c + 2 < CHUNKS:
                     load_x(c + 2, (nc.sync,))
-                    load_angles(c + 2)
+                    if c + 3 < CHUNKS:
+                        load_angles(c + 3)
                 transpose(q + 3)
             if q == -3:
                 gains_to_psum()
                 build_table(True, 0)
                 build_table(True, 1)
+                build_cos(False, VECTOR_HEAD_STEPS * STEP_TILES, (TABLE_LEAD - VECTOR_HEAD_STEPS) * STEP_TILES)
+                build_sin(False, VECTOR_HEAD_STEPS * STEP_TILES, (TABLE_LEAD - VECTOR_HEAD_STEPS) * STEP_TILES)
             if q >= 0:
                 multiply(q)
                 quantise_next(q)
@@ -307,6 +310,3 @@ def tile_qwen3nextattentionforengine_pa_t_kernel(
                 quantise_next(q)
                 if q == -2:
                     build_table(True, 2)
-                if q == -1:
-                    nc.vector.tensor_copy(out=gains_late[:], in_=gains[:].rearrange("p s c d -> p s (c d)"))
-                    build_table(False, 3)

@@ -35,8 +35,8 @@ BANK_GROUPS = GROUPS // STEP_BANKS
 CHUNK = 8
 CHUNKS = TILES // CHUNK
 CHUNK_STEPS = CHUNK // STEP_TILES
-TABLE_LEAD = 6
-VECTOR_HEAD_STEPS = 3
+TABLE_LEAD = 5
+HEAD_STEPS = 4
 GPSIMD_COS_TILES = 2
 
 FLOPS = 2 * TOKENS * K * N_OUT
@@ -140,12 +140,20 @@ def tile_qwen3nextattentionforengine_pa_t_kernel(
                 stop=True,
             )
 
+        gains_late = const.tile([P, SIDES, 2 * D], BF16, name="gains_late")
+        factors_of = {
+            (True, True): gains[:].rearrange("p s c d -> p s (c d)"),
+            (True, False): gains_ps[:],
+            (False, True): gains_late[:],
+            (False, False): gains_late[:],
+        }
+
         tables = const.tile([P, TILES, SIDES, 2, D], F32, name="tables")
 
         def build_cos(on_vector, first, count):
             shape = [P, count, SIDES, D]
             engine = nc.vector if on_vector else nc.gpsimd
-            factors = gains_ps[:] if on_vector else gains[:].rearrange("p s c d -> p s (c d)")
+            factors = factors_of[(on_vector, first < HEAD_STEPS * STEP_TILES)]
             engine.tensor_tensor(
                 out=tables[:, first : first + count, :, 0, :],
                 in0=angles[:, 0, first : first + count, :].unsqueeze(2).to_broadcast(shape),
@@ -156,7 +164,7 @@ def tile_qwen3nextattentionforengine_pa_t_kernel(
         def build_sin(on_vector, first, count):
             shape = [P, count, SIDES, HALF]
             engine = nc.vector if on_vector else nc.gpsimd
-            factors = gains_ps[:] if on_vector else gains[:].rearrange("p s c d -> p s (c d)")
+            factors = factors_of[(on_vector, first < HEAD_STEPS * STEP_TILES)]
             for a in range(2):
                 engine.tensor_tensor(
                     out=tables[:, first : first + count, :, 1, a * HALF : (a + 1) * HALF],
@@ -295,8 +303,6 @@ def tile_qwen3nextattentionforengine_pa_t_kernel(
                 gains_to_psum()
                 build_table(True, 0)
                 build_table(True, 1)
-                build_cos(False, VECTOR_HEAD_STEPS * STEP_TILES, (TABLE_LEAD - VECTOR_HEAD_STEPS) * STEP_TILES)
-                build_sin(False, VECTOR_HEAD_STEPS * STEP_TILES, (TABLE_LEAD - VECTOR_HEAD_STEPS) * STEP_TILES)
             if q >= 0:
                 multiply(q)
                 quantise_next(q)
@@ -310,3 +316,7 @@ def tile_qwen3nextattentionforengine_pa_t_kernel(
                 quantise_next(q)
                 if q == -2:
                     build_table(True, 2)
+                    build_table(True, 3)
+                if q == -1:
+                    nc.vector.tensor_copy(out=gains_late[:], in_=gains[:].rearrange("p s c d -> p s (c d)"))
+                    build_table(False, 4)

@@ -36,7 +36,6 @@ CHUNK = 8
 CHUNKS = TILES // CHUNK
 CHUNK_STEPS = CHUNK // STEP_TILES
 TABLE_LEAD = 5
-HEAD_STEPS = 4
 GPSIMD_COS_TILES = 2
 
 FLOPS = 2 * TOKENS * K * N_OUT
@@ -140,20 +139,13 @@ def tile_qwen3nextattentionforengine_pa_t_kernel(
                 stop=True,
             )
 
-        gains_late = const.tile([P, SIDES, 2 * D], BF16, name="gains_late")
-        factors_of = {
-            (True, True): gains[:].rearrange("p s c d -> p s (c d)"),
-            (True, False): gains_ps[:],
-            (False, True): gains_late[:],
-            (False, False): gains_late[:],
-        }
+        gains_sb = gains[:].rearrange("p s c d -> p s (c d)")
+        gains_late = [const.tile([P, SIDES, 2 * D], BF16, name="gains_late%d" % n) for n in range(2)]
 
         tables = const.tile([P, TILES, SIDES, 2, D], F32, name="tables")
 
-        def build_cos(on_vector, first, count):
+        def build_cos(engine, factors, first, count):
             shape = [P, count, SIDES, D]
-            engine = nc.vector if on_vector else nc.gpsimd
-            factors = factors_of[(on_vector, first < HEAD_STEPS * STEP_TILES)]
             engine.tensor_tensor(
                 out=tables[:, first : first + count, :, 0, :],
                 in0=angles[:, 0, first : first + count, :].unsqueeze(2).to_broadcast(shape),
@@ -161,23 +153,19 @@ def tile_qwen3nextattentionforengine_pa_t_kernel(
                 op=ALU.mult,
             )
 
-        def build_sin(on_vector, first, count):
+        def build_sin(engine, factors, first, count, a):
             shape = [P, count, SIDES, HALF]
-            engine = nc.vector if on_vector else nc.gpsimd
-            factors = factors_of[(on_vector, first < HEAD_STEPS * STEP_TILES)]
-            for a in range(2):
-                engine.tensor_tensor(
-                    out=tables[:, first : first + count, :, 1, a * HALF : (a + 1) * HALF],
-                    in0=angles[:, 1, first : first + count, (1 - a) * HALF : (2 - a) * HALF]
-                    .unsqueeze(2)
-                    .to_broadcast(shape),
-                    in1=factors[:, :, D + a * HALF : D + (a + 1) * HALF].unsqueeze(1).to_broadcast(shape),
-                    op=ALU.mult,
-                )
+            engine.tensor_tensor(
+                out=tables[:, first : first + count, :, 1, a * HALF : (a + 1) * HALF],
+                in0=angles[:, 1, first : first + count, (1 - a) * HALF : (2 - a) * HALF].unsqueeze(2).to_broadcast(shape),
+                in1=factors[:, :, D + a * HALF : D + (a + 1) * HALF].unsqueeze(1).to_broadcast(shape),
+                op=ALU.mult,
+            )
 
-        def build_table(on_vector, q):
-            build_cos(on_vector, q * STEP_TILES, STEP_TILES)
-            build_sin(on_vector, q * STEP_TILES, STEP_TILES)
+        def build_table(engine, factors, q):
+            build_cos(engine, factors, q * STEP_TILES, STEP_TILES)
+            build_sin(engine, factors, q * STEP_TILES, STEP_TILES, 0)
+            build_sin(engine, factors, q * STEP_TILES, STEP_TILES, 1)
 
         transposed = {}
 
@@ -235,12 +223,12 @@ def tile_qwen3nextattentionforengine_pa_t_kernel(
             heads = projected[q]
             sumsq = stat_pool.tile([P, GROUPS], F32, name="sumsq")
             rstd = stat_pool.tile([P, GROUPS], F32, name="rstd")
+            squares = stat_pool.tile([P, GROUPS, D], F32, name="squares")
             for b in range(STEP_BANKS):
                 bank = slice(b * BANK_GROUPS, (b + 1) * BANK_GROUPS)
                 for g in range(b * BANK_GROUPS, (b + 1) * BANK_GROUPS):
-                    squares = stat_pool.tile([P, D], F32, name="squares")
                     nc.scalar.activation(
-                        out=squares[:], in_=heads[g], func=ACT.Square, accum_out=sumsq[:, g : g + 1]
+                        out=squares[:, g, :], in_=heads[g], func=ACT.Square, accum_out=sumsq[:, g : g + 1]
                     )
                 nc.scalar.activation(
                     out=rstd[:, bank], in_=sumsq[:, bank], func=ACT.Abs_reciprocal_sqrt, bias=eps[:, 0:1], scale=1.0 / D
@@ -301,22 +289,29 @@ def tile_qwen3nextattentionforengine_pa_t_kernel(
                 transpose(q + 3)
             if q == -3:
                 gains_to_psum()
-                build_table(True, 0)
-                build_table(True, 1)
+                build_table(nc.vector, gains_sb, 0)
+                build_table(nc.vector, gains_sb, 1)
             if q >= 0:
                 multiply(q)
                 quantise_next(q)
                 add_and_store(nc.gpsimd if q + 1 < STEPS else nc.vector, q)
                 if q + TABLE_LEAD < STEPS:
                     first = (q + TABLE_LEAD) * STEP_TILES
-                    build_cos(True, first, STEP_TILES - GPSIMD_COS_TILES)
-                    build_sin(True, first, STEP_TILES)
-                    build_cos(False, first + STEP_TILES - GPSIMD_COS_TILES, GPSIMD_COS_TILES)
+                    build_cos(nc.vector, gains_ps[:], first, STEP_TILES - GPSIMD_COS_TILES)
+                    build_sin(nc.vector, gains_ps[:], first, STEP_TILES, 0)
+                    build_sin(nc.vector, gains_ps[:], first, STEP_TILES, 1)
+                    build_cos(nc.gpsimd, gains_late[1][:], first + STEP_TILES - GPSIMD_COS_TILES, GPSIMD_COS_TILES)
+                if q == 0:
+                    build_sin(nc.vector, gains_ps[:], 4 * STEP_TILES, STEP_TILES, 1)
             else:
                 quantise_next(q)
                 if q == -2:
-                    build_table(True, 2)
-                    build_table(True, 3)
+                    nc.vector.tensor_copy(out=gains_late[0][:], in_=gains_sb)
+                    build_cos(nc.gpsimd, gains_late[0][:], 3 * STEP_TILES, STEP_TILES)
+                    build_table(nc.vector, gains_ps[:], 2)
+                    build_sin(nc.vector, gains_ps[:], 3 * STEP_TILES, STEP_TILES, 0)
+                    build_sin(nc.vector, gains_ps[:], 3 * STEP_TILES, STEP_TILES, 1)
                 if q == -1:
-                    nc.vector.tensor_copy(out=gains_late[:], in_=gains[:].rearrange("p s c d -> p s (c d)"))
-                    build_table(False, 4)
+                    nc.vector.tensor_copy(out=gains_late[1][:], in_=gains_sb)
+                    build_cos(nc.gpsimd, gains_late[1][:], 4 * STEP_TILES, STEP_TILES)
+                    build_sin(nc.gpsimd, gains_late[1][:], 4 * STEP_TILES, STEP_TILES, 0)

@@ -36,7 +36,6 @@ CHUNK = 8
 CHUNKS = TILES // CHUNK
 CHUNK_STEPS = CHUNK // STEP_TILES
 TABLE_LEAD = 5
-GPSIMD_COS_TILES = 2
 
 FLOPS = 2 * TOKENS * K * N_OUT
 
@@ -289,29 +288,29 @@ def tile_qwen3nextattentionforengine_pa_t_kernel(
                 transpose(q + 3)
             if q == -3:
                 gains_to_psum()
-                build_table(nc.vector, gains_sb, 0)
-                build_table(nc.vector, gains_sb, 1)
+                build_cos(nc.vector, gains_sb, 0, 2 * STEP_TILES)
+                build_sin(nc.vector, gains_sb, 0, 2 * STEP_TILES, 0)
+                build_sin(nc.vector, gains_sb, 0, 2 * STEP_TILES, 1)
             if q >= 0:
                 multiply(q)
                 quantise_next(q)
                 add_and_store(nc.gpsimd if q + 1 < STEPS else nc.vector, q)
                 if q + TABLE_LEAD < STEPS:
                     first = (q + TABLE_LEAD) * STEP_TILES
-                    build_cos(nc.vector, gains_ps[:], first, STEP_TILES - GPSIMD_COS_TILES)
-                    build_sin(nc.vector, gains_ps[:], first, STEP_TILES, 0)
-                    build_sin(nc.vector, gains_ps[:], first, STEP_TILES, 1)
-                    build_cos(nc.gpsimd, gains_late[1][:], first + STEP_TILES - GPSIMD_COS_TILES, GPSIMD_COS_TILES)
-                if q == 0:
-                    build_sin(nc.vector, gains_ps[:], 4 * STEP_TILES, STEP_TILES, 1)
+                    if q > 0:
+                        build_cos(nc.vector, gains_ps[:], first, STEP_TILES)
+                        build_sin(nc.vector, gains_ps[:], first, STEP_TILES, 0)
+                    build_sin(nc.gpsimd, gains_late[1][:], first, STEP_TILES, 1)
             else:
                 quantise_next(q)
                 if q == -2:
                     nc.vector.tensor_copy(out=gains_late[0][:], in_=gains_sb)
                     build_cos(nc.gpsimd, gains_late[0][:], 3 * STEP_TILES, STEP_TILES)
-                    build_table(nc.vector, gains_ps[:], 2)
-                    build_sin(nc.vector, gains_ps[:], 3 * STEP_TILES, STEP_TILES, 0)
-                    build_sin(nc.vector, gains_ps[:], 3 * STEP_TILES, STEP_TILES, 1)
+                    build_cos(nc.vector, gains_ps[:], 2 * STEP_TILES, STEP_TILES)
+                    build_sin(nc.vector, gains_ps[:], 2 * STEP_TILES, 2 * STEP_TILES, 0)
+                    build_sin(nc.vector, gains_ps[:], 2 * STEP_TILES, 2 * STEP_TILES, 1)
                 if q == -1:
                     nc.vector.tensor_copy(out=gains_late[1][:], in_=gains_sb)
-                    build_cos(nc.gpsimd, gains_late[1][:], 4 * STEP_TILES, STEP_TILES)
-                    build_sin(nc.gpsimd, gains_late[1][:], 4 * STEP_TILES, STEP_TILES, 0)
+                    build_table(nc.gpsimd, gains_late[1][:], 4)
+                    build_cos(nc.vector, gains_ps[:], TABLE_LEAD * STEP_TILES, STEP_TILES)
+                    build_sin(nc.vector, gains_ps[:], TABLE_LEAD * STEP_TILES, STEP_TILES, 0)

@@ -102,6 +102,8 @@ def tile_qwen3nextattentionforengine_pa_t_kernel(
 
         eps = const.tile([P, 1], F32, name="eps")
         nc.vector.memset(eps[:], EPS)
+        first_rstd = const.tile([P, 1], F32, name="first_rstd")
+        nc.scalar.activation(out=first_rstd[:], in_=eps[:], func=ACT.Abs_reciprocal_sqrt)
 
         w_words = const.tile([P, 2 * N_OUT], U8, name="w_words", align_bytes=64)
         for s, words in enumerate((Wq_query_words, Wk_words)):

from contextlib import ExitStack

import concourse.mybir as mybir
from concourse.masks import make_identity

F32 = mybir.dt.float32
BF16 = mybir.dt.bfloat16
U8 = mybir.dt.uint8
U32 = mybir.dt.uint32
I32 = mybir.dt.int32
FP8X4 = mybir.dt.float8_e4m3fn_x4
FP4X4 = mybir.dt.float4_e2m1fn_x4
ALU = mybir.AluOpType
ACT = mybir.ActivationFunctionType

P = 128
PACK = 4
K = P * PACK
TOKENS = 4 * 2048
TILES = TOKENS // P
HEADS = 2
D = 64
HALF = D // 2
SIDES = 2
N_SIDE = HEADS * D
N_OUT = SIDES * N_SIDE
EPS = 1e-6

BANK_TILES = 2
STEP_TILES = 4
STEP_BANKS = STEP_TILES // BANK_TILES
STEPS = TILES // STEP_TILES
GROUPS = STEP_TILES * SIDES * HEADS
BANK_GROUPS = GROUPS // STEP_BANKS
CHUNK = 8
CHUNKS = TILES // CHUNK
CHUNK_STEPS = CHUNK // STEP_TILES
TABLE_LEAD = 5

FLOPS = 2 * TOKENS * K * N_OUT


def tile_qwen3nextattentionforengine_pa_t_kernel(
    tc,
    hidden_states,
    cos,
    sin,
    Wq_query_words,
    Wq_query_scales,
    Wk_words,
    Wk_scales,
    q_norm_w,
    k_norm_w,
    out_0,
    out_1,
):
    nc = tc.nc
    x_view = hidden_states.rearrange("b (q i) k -> (b q) i k", i=TILES)
    cos_view = cos.rearrange("b (q i) d -> (b q) i d", i=TILES)
    sin_view = sin.rearrange("b (q i) d -> (b q) i d", i=TILES)
    out_views = (
        out_0.rearrange("b (q i) h d -> (b q) i (h d)", i=TILES),
        out_1.rearrange("b (q i) h d -> (b q) i (h d)", i=TILES),
    )

    with ExitStack() as pools:
        const = pools.enter_context(tc.tile_pool(name="const", bufs=1))
        x_pool = pools.enter_context(tc.tile_pool(name="x_pool", bufs=3))
        quant_pool = pools.enter_context(tc.tile_pool(name="quant_pool", bufs=3))
        stat_pool = pools.enter_context(tc.tile_pool(name="stat_pool", bufs=3))
        prod_pool = pools.enter_context(tc.tile_pool(name="prod_pool", bufs=3))
        res_pool = pools.enter_context(tc.tile_pool(name="res_pool", bufs=3))
        xt_psum = pools.enter_context(tc.psum_pool(name="xt_psum", bufs=3))
        v_psum = pools.enter_context(tc.psum_pool(name="v_psum", bufs=4))
        gain_psum = pools.enter_context(tc.psum_pool(name="gain_psum", bufs=1))
        pools.enter_context(tc.manual_schedule())

        x_chunks = {}

        def load_x(c, queues):
            x_sb = x_pool.tile([P, CHUNK, K], BF16, name="x_sb")
            size = CHUNK // len(queues)
            for piece, queue in enumerate(queues):
                tiles = slice(piece * size, (piece + 1) * size)
                queue.dma_start(out=x_sb[:, tiles, :], in_=x_view[:, c * CHUNK : (c + 1) * CHUNK, :][:, tiles, :])
            x_chunks[c] = x_sb

        angles = const.tile([P, 2, TILES, D], BF16, name="angles")

        def load_angles(c):
            tiles = slice(c * CHUNK, (c + 1) * CHUNK)
            nc.sync.dma_start(out=angles[:, 0, tiles, :], in_=cos_view[:, tiles, :])
            nc.sync.dma_start(out=angles[:, 1, tiles, :], in_=sin_view[:, tiles, :])

        ident = const.tile([P, P], F32, name="ident")
        make_identity(nc, ident[:])
        load_x(0, (nc.sync, nc.gpsimd))
        gains = const.tile([P, SIDES, 2, D], BF16, name="gains")
        nc.scalar.dma_start(out=gains[:, 0, 0, :], in_=q_norm_w.partition_broadcast(P))
        nc.scalar.dma_start(out=gains[:, 1, 0, :], in_=k_norm_w.partition_broadcast(P))
        load_angles(0)

        eps = const.tile([P, 1], F32, name="eps")
        nc.vector.memset(eps[:], EPS)
        first_rstd = const.tile([P, 1], F32, name="first_rstd")
        nc.scalar.activation(out=first_rstd[:], in_=eps[:], func=ACT.Abs_reciprocal_sqrt)

        w_words = const.tile([P, 2 * N_OUT], U8, name="w_words", align_bytes=64)
        for s, words in enumerate((Wq_query_words, Wk_words)):
            nc.sync.dma_start(
                out=w_words[:, s * 2 * N_SIDE : (s + 1) * 2 * N_SIDE].bitcast(I32),
                in_=words.rearrange("g p n -> (g p) n").bitcast(I32),
            )
        w_plane = const.tile([P, N_OUT], U8, name="w_plane", align_bytes=64)
        nc.vector.memset(w_plane[:].bitcast(I32), 0)
        for s, scales in enumerate((Wq_query_scales, Wk_scales)):
            rows = scales.rearrange("g q n -> (g q) n")
            for quad in range(4):
                nc.sync.dma_start(
                    out=w_plane[32 * quad : 32 * quad + 4, s * N_SIDE : (s + 1) * N_SIDE].bitcast(I32),
                    in_=rows[4 * quad : 4 * quad + 4, :].bitcast(I32),
                )
        load_angles(1)
        load_angles(2)
        load_x(1, (nc.sync,))

        ident_bf = const.tile([P, P], BF16, name="ident_bf")
        nc.vector.tensor_copy(out=ident_bf[:], in_=ident[:])
        nc.vector.tensor_copy(out=gains[:, :, 1, 0:HALF], in_=gains[:, :, 0, 0:HALF])
        nc.vector.tensor_scalar_mul(out=gains[:, :, 1, HALF:D], in0=gains[:, :, 0, HALF:D], scalar1=-1.0)

        gains_ps = gain_psum.tile([P, SIDES, 2 * D], F32, name="gains_ps")

        def gains_to_psum():
            nc.tensor.matmul(
                out=gains_ps[:].rearrange("p s n -> p (s n)"),
                lhsT=ident_bf[:],
                rhs=gains[:].rearrange("p s c d -> p (s c d)"),
                start=True,
                stop=True,
            )

        gains_sb = gains[:].rearrange("p s c d -> p s (c d)")
        gains_late = [const.tile([P, SIDES, 2 * D], BF16, name="gains_late%d" % n) for n in range(2)]

        tables = const.tile([P, TILES, SIDES, 2, D], F32, name="tables")

        def build_cos(engine, factors, first, count):
            shape = [P, count, SIDES, D]
            engine.tensor_tensor(
                out=tables[:, first : first + count, :, 0, :],
                in0=angles[:, 0, first : first + count, :].unsqueeze(2).to_broadcast(shape),
                in1=factors[:, :, 0:D].unsqueeze(1).to_broadcast(shape),
                op=ALU.mult,
            )

        def build_sin(engine, factors, first, count, a):
            shape = [P, count, SIDES, HALF]
            engine.tensor_tensor(
                out=tables[:, first : first + count, :, 1, a * HALF : (a + 1) * HALF],
                in0=angles[:, 1, first : first + count, (1 - a) * HALF : (2 - a) * HALF].unsqueeze(2).to_broadcast(shape),
                in1=factors[:, :, D + a * HALF : D + (a + 1) * HALF].unsqueeze(1).to_broadcast(shape),
                op=ALU.mult,
            )

        def build_table(engine, factors, q):
            build_cos(engine, factors, q * STEP_TILES, STEP_TILES)
            build_sin(engine, factors, q * STEP_TILES, STEP_TILES, 0)
            build_sin(engine, factors, q * STEP_TILES, STEP_TILES, 1)

        transposed = {}

        def transpose(q):
            x_sb = x_chunks[q // CHUNK_STEPS]
            first = (q % CHUNK_STEPS) * STEP_TILES
            grouped = quant_pool.tile([P, STEP_BANKS, BANK_TILES * P * PACK], BF16, name="grouped", align_bytes=64)
            for b in range(STEP_BANKS):
                xt = xt_psum.tile([P, BANK_TILES, 2, P], F32, name="xt")
                for t in range(BANK_TILES):
                    words = x_sb[:, first + b * BANK_TILES + t, :].bitcast(F32)
                    for u in range(2):
                        nc.tensor.transpose(xt[:, t, u, :], words[:, u : K // 2 : 2], ident[:])
                nc.scalar.copy(
                    out=grouped[:, b, :].bitcast(F32).rearrange("p (t r u) -> p t r u", t=BANK_TILES, u=2),
                    in_=xt[:].rearrange("p t u r -> p t r u"),
                )
            transposed[q] = grouped

        quantised = {}

        def quantise(q):
            grouped = transposed.pop(q)
            codes = quant_pool.tile([P, STEP_TILES * P], U32, name="codes", align_bytes=64)
            plane = quant_pool.tile([P, STEP_TILES * P], U8, name="plane", align_bytes=64)
            nc.vector.quantize_mx(
                out=codes[:].bitcast(FP8X4), scales=plane[:], in_=grouped[:].rearrange("p b n -> p (b n)")
            )
            quantised[q] = (codes, plane)

        projected = {}

        def project(q):
            codes, plane = quantised.pop(q)
            heads = []
            for b in range(STEP_BANKS):
                v = v_psum.tile([P, BANK_TILES, N_OUT], F32, name="v")
                for t in range(BANK_TILES):
                    tokens = slice((b * BANK_TILES + t) * P, (b * BANK_TILES + t + 1) * P)
                    nc.tensor.matmul_mx(
                        out=v[:, t, :],
                        lhsT=codes[:, tokens].bitcast(FP8X4),
                        lhsT_scale=plane[:, tokens],
                        rhs=w_words[:].bitcast(FP4X4),
                        rhs_scale=w_plane[:],
                        start=True,
                        stop=True,
                    )
                    heads.extend(v[:, t, n : n + D] for n in range(0, N_OUT, D))
            projected[q] = heads

        measured = {}

        def measure(q):
            heads = projected[q]
            sumsq = stat_pool.tile([P, GROUPS], F32, name="sumsq")
            rstd = stat_pool.tile([P, GROUPS], F32, name="rstd")
            squares = stat_pool.tile([P, GROUPS, D], F32, name="squares")
            for b in range(STEP_BANKS):
                bank = slice(b * BANK_GROUPS, (b + 1) * BANK_GROUPS)
                for g in range(b * BANK_GROUPS, (b + 1) * BANK_GROUPS):
                    nc.scalar.activation(
                        out=squares[:, g, :], in_=heads[g], func=ACT.Square, accum_out=sumsq[:, g : g + 1]
                    )
                nc.scalar.activation(
                    out=rstd[:, bank], in_=sumsq[:, bank], func=ACT.Abs_reciprocal_sqrt, bias=eps[:, 0:1], scale=1.0 / D
                )
            measured[q] = rstd

        products = {}

        def multiply(q):
            heads = projected.pop(q)
            rstd = measured.pop(q)
            table = tables[:, q * STEP_TILES : (q + 1) * STEP_TILES]
            prod = prod_pool.tile([P, SIDES, STEP_TILES, HEADS, 2, D], F32, name="prod")
            for i in range(STEP_TILES):
                for s in range(SIDES):
                    for h in range(HEADS):
                        g = (i * SIDES + s) * HEADS + h
                        nc.vector.scalar_tensor_tensor(
                            out=prod[:, s, i, h, :, :],
                            in0=heads[g].unsqueeze(1).to_broadcast([P, 2, D]),
                            scalar=rstd[:, g : g + 1],
                            in1=table[:, i, s, :, :],
                            op0=ALU.mult,
                            op1=ALU.mult,
                        )
            products[q] = prod

        def add_and_store(engine, q):
            prod = products.pop(q)
            res = res_pool.tile([P, SIDES, STEP_TILES, HEADS, 2, HALF], F32, name="res")
            halves = prod[:].rearrange("p s i h c (a d) -> p (s i h) c a d", a=2)
            engine.tensor_tensor(
                out=res[:].rearrange("p s i h a d -> p (s i h) a d"),
                in0=halves[:, :, 0, :, :],
                in1=halves[:, :, 1, ::-1, :],
                op=ALU.add,
            )
            for s in range(SIDES):
                nc.sync.dma_start(
                    out=out_views[s][:, q * STEP_TILES : (q + 1) * STEP_TILES, :],
                    in_=res[:, s].rearrange("p i h a d -> p i (h a d)"),
                )

        def quantise_next(q):
            if 0 <= q + 2 < STEPS:
                quantise(q + 2)

        for q in range(-3, STEPS):
            if 0 <= q + 1 < STEPS:
                project(q + 1)
                measure(q + 1)
            if q + 3 < STEPS:
                c = (q + 3) // CHUNK_STEPS
                if (q + 3) % CHUNK_STEPS == 0 and c + 2 < CHUNKS:
                    load_x(c + 2, (nc.sync,))
                    if c + 3 < CHUNKS:
                        load_angles(c + 3)
                transpose(q + 3)
            if q == -3:
                gains_to_psum()
                build_cos(nc.vector, gains_sb, 0, 2 * STEP_TILES)
                build_sin(nc.vector, gains_sb, 0, 2 * STEP_TILES, 0)
                build_sin(nc.vector, gains_sb, 0, 2 * STEP_TILES, 1)
            if q >= 0:
                multiply(q)
                quantise_next(q)
                add_and_store(nc.gpsimd if q + 1 < STEPS else nc.vector, q)
                if q + TABLE_LEAD < STEPS:
                    first = (q + TABLE_LEAD) * STEP_TILES
                    if q > 0:
                        build_cos(nc.vector, gains_ps[:], first, STEP_TILES)
                        build_sin(nc.vector, gains_ps[:], first, STEP_TILES, 0)
                    build_sin(nc.gpsimd, gains_late[1][:], first, STEP_TILES, 1)
            else:
                quantise_next(q)
                if q == -2:
                    nc.vector.tensor_copy(out=gains_late[0][:], in_=gains_sb)
                    build_cos(nc.gpsimd, gains_late[0][:], 3 * STEP_TILES, STEP_TILES)
                    build_cos(nc.vector, gains_ps[:], 2 * STEP_TILES, STEP_TILES)
                    build_sin(nc.vector, gains_ps[:], 2 * STEP_TILES, 2 * STEP_TILES, 0)
                    build_sin(nc.vector, gains_ps[:], 2 * STEP_TILES, 2 * STEP_TILES, 1)
                if q == -1:
                    nc.vector.tensor_copy(out=gains_late[1][:], in_=gains_sb)
                    build_table(nc.gpsimd, gains_late[1][:], 4)
                    build_cos(nc.vector, gains_ps[:], TABLE_LEAD * STEP_TILES, STEP_TILES)
                    build_sin(nc.vector, gains_ps[:], TABLE_LEAD * STEP_TILES, STEP_TILES, 0)
